import numpy as np
import ml_dtypes


def mxq(x, axis, fmt="e4m3"):
    dtype, down = {"e4m3": (ml_dtypes.float8_e4m3fn, 7), "e5m2": (ml_dtypes.float8_e5m2, 14)}[fmt]
    v = np.moveaxis(np.asarray(x, np.float32).astype(ml_dtypes.bfloat16).astype(np.float64), axis, -1)
    blocks = v.reshape(v.shape[:-1] + (-1, 32))
    amax = np.abs(blocks).max(-1, keepdims=True)
    byte = np.maximum(np.where(amax > 0, np.frexp(amax)[1] - 1 + 127, 0) - down, 1)
    scale = np.exp2(byte - 127.0)
    codes = (blocks / scale).astype(np.float32).astype(dtype).astype(np.float64)
    return np.moveaxis((codes * scale).reshape(v.shape), -1, axis)


WIDE = False


def mx_kscale(k):
    if not WIDE:
        return np.ones(k)
    levels = np.array([10, -10, 5, -5, 0])
    if k % 512:
        return np.exp2(np.random.permutation(np.resize(levels, k // 32))).repeat(32)
    a = np.empty((k // 512, 16))
    for p in range(k // 512):
        a[p, :8] = np.random.permutation(np.resize(levels, 8))
        for g in range(8):
            far = levels[np.abs(levels - a[p, g]) >= 10]
            a[p, g + 8] = far[np.random.randint(len(far))]
    return np.exp2(a.ravel()).repeat(32)


BF16 = ml_dtypes.bfloat16


def bf(x):
    return np.asarray(x, np.float32).astype(BF16)


def f64(x):
    return np.asarray(x).astype(np.float64)


B, I, H = 128, 2048, 2048
EPS = 1e-5


def sigmoid(v):
    return 1.0 / (1.0 + np.exp(-v))


def ln(v, g, b):
    m = v.mean(-1, keepdims=True)
    var = np.square(v - m).mean(-1, keepdims=True)
    return (v - m) / np.sqrt(var + EPS) * g + b


def setup_inputs():
    s, t = mx_kscale(I), mx_kscale(H)
    d = {"x": bf(np.random.standard_normal((B, I)) * s), "h": bf(np.random.standard_normal((B, H)) * t)}
    for g in ("i", "c"):
        d["W" + g + "_w"] = bf(np.random.standard_normal((H, I)) / np.sqrt(I) / s[None, :])
        d["W" + g + "_b"] = bf(np.random.standard_normal(H) * 0.5)
        d["U" + g + "_w"] = bf(np.random.standard_normal((H, H)) / np.sqrt(H) / t[None, :])
        d["ln" + g + "_g"] = bf(1.0 + 0.2 * np.random.standard_normal(H))
        d["ln" + g + "_b"] = bf(0.2 * np.random.standard_normal(H))
    return d


def reference(x, h, Wi_w, Wi_b, Ui_w, lni_g, lni_b, Wc_w, Wc_b, Uc_w, lnc_g, lnc_b):
    xq = mxq(f64(x), 1, "e4m3")
    hq = mxq(f64(h), 1, "e4m3")
    pre_i = (xq @ mxq(f64(Wi_w), 1, "e4m3").T) + f64(Wi_b) + (hq @ mxq(f64(Ui_w), 1, "e4m3").T)
    pre_c = (xq @ mxq(f64(Wc_w), 1, "e4m3").T) + f64(Wc_b) + (hq @ mxq(f64(Uc_w), 1, "e4m3").T)
    i = sigmoid(ln(pre_i, f64(lni_g), f64(lni_b)))
    c_tilde = np.tanh(ln(pre_c, f64(lnc_g), f64(lnc_b)))
    return i * c_tilde

@@ -1,0 +1,285 @@
+from contextlib import ExitStack
+
+import concourse.mybir as mybir
+from concourse.masks import make_identity
+
+F32 = mybir.dt.float32
+BF16 = mybir.dt.bfloat16
+U32 = mybir.dt.uint32
+U8 = mybir.dt.uint8
+FP8X4 = mybir.dt.float8_e4m3fn_x4
+ALU = mybir.AluOpType
+ACT = mybir.ActivationFunctionType
+
+P = 128
+FEATURES = 2048
+HIDDEN = 2048
+GATES = 2
+OPERANDS = 2
+PACK = 4
+K_PASS = P * PACK
+PASSES = FEATURES // K_PASS
+PASS_WORDS = K_PASS // 2
+ROW_WORDS = FEATURES // 2
+N_TILE = 2 * P
+GROUPS = HIDDEN // N_TILE
+ROUNDS = GATES * GROUPS * OPERANDS
+BANK_WORDS = 512
+PIECE = 512
+PIECES = HIDDEN // PIECE
+STATS = 6
+EPS = 1e-5
+
+RAW_BUFS = 8
+MX_LAG = 2
+VECTOR_EVERY = 8
+VECTOR_BANK = 5
+
+FLOPS = 2 * P * GATES * HIDDEN * OPERANDS * FEATURES
+
+
+def words_onto_partitions(nc, psum, identity, blocks, dest, copy):
+    bank = psum.tile([P, 2, 2, P], F32, tag="bank")
+    for a in range(2):
+        for u in range(2):
+            nc.tensor.transpose(bank[:, a, u, :], blocks[a][:, u : PASS_WORDS : 2], identity)
+    copy(
+        out=dest.rearrange("p (a r u) -> p a r u", a=2, u=2),
+        in_=bank[:].rearrange("p a u r -> p a r u"),
+    )
+
+
+def tile_layernormlstmcell_pa_kernel(
+    tc, x, h, Wi_w, Wi_b, Ui_w, lni_g, lni_b, Wc_w, Wc_b, Uc_w, lnc_g, lnc_b, out
+):
+    nc = tc.nc
+    weights = ((Wi_w, Ui_w), (Wc_w, Uc_w))
+    vector_rows = (Wi_b, Wc_b, lni_g, lni_b, lnc_g, lnc_b)
+    functions = (ACT.Sigmoid, ACT.Tanh)
+
+    with ExitStack() as ctx:
+        ctx.enter_context(tc.manual_schedule())
+        keep = ctx.enter_context(tc.tile_pool(name="keep", bufs=1))
+        raw_pool = ctx.enter_context(tc.tile_pool(name="raw", bufs=RAW_BUFS))
+        grouped_pool = ctx.enter_context(tc.tile_pool(name="grouped", bufs=4))
+        mx_pool = ctx.enter_context(tc.tile_pool(name="mx", bufs=MX_LAG + 2))
+        work_psum = ctx.enter_context(tc.psum_pool(name="work_psum", bufs=6))
+        acc_psum = ctx.enter_context(tc.psum_pool(name="acc_psum", bufs=2))
+
+        a_raw = []
+        for s, operand in enumerate((x, h)):
+            rows = keep.tile([P, FEATURES], BF16, name="a_raw%d" % s)
+            nc.sync.dma_start(out=rows[:], in_=operand)
+            a_raw.append(rows)
+
+        identity_words = keep.tile([P, P], F32)
+        make_identity(nc, identity_words[:])
+        identity_bf16 = keep.tile([P, P], BF16)
+        make_identity(nc, identity_bf16[:])
+
+        vectors = keep.tile([P, HIDDEN], BF16)
+        nc.vector.memset(vectors[:], 0.0)
+        for row, vector in enumerate(vector_rows):
+            nc.gpsimd.dma_start(out=vectors[row : row + 1, :], in_=vector.unsqueeze(0))
+        minus_half = keep.tile([P, 1], F32)
+        nc.vector.memset(minus_half[:], -0.5)
+
+        table_warmer = keep.tile([P, 1], F32)
+        nc.vector.memset(table_warmer[:], 0.0)
+        nc.scalar.activation(out=table_warmer[:], in_=table_warmer[:], func=ACT.Sigmoid)
+
+        a_codes = keep.tile([P, OPERANDS * PASSES * P], U32, align_bytes=64)
+        a_scales = keep.tile([P, OPERANDS * PASSES * P], U8, align_bytes=64)
+        for s in range(OPERANDS):
+            a_words = a_raw[s][:].bitcast(F32)
+            a_grouped = keep.tile([P, PASSES * P * PACK], BF16, align_bytes=64, name="a_grouped%d" % s)
+            a_grouped_words = a_grouped[:].bitcast(F32)
+            for pair in range(PASSES // 2):
+                first = 2 * pair * PASS_WORDS
+                words_onto_partitions(
+                    nc,
+                    work_psum,
+                    identity_words[:],
+                    [a_words[:, first + a * PASS_WORDS : first + (a + 1) * PASS_WORDS] for a in range(2)],
+                    a_grouped_words[:, first : first + BANK_WORDS],
+                    nc.vector.tensor_copy if pair % 2 else nc.scalar.copy,
+                )
+            a_cols = slice(s * PASSES * P, (s + 1) * PASSES * P)
+            nc.vector.quantize_mx(
+                out=a_codes[:, a_cols].bitcast(FP8X4), scales=a_scales[:, a_cols], in_=a_grouped[:]
+            )
+
+        def spread_row(dest, row, cols):
+            nc.tensor.matmul(
+                out=dest,
+                lhsT=identity_bf16[:, row : row + 1].to_broadcast([P, P]),
+                rhs=vectors[:, cols],
+                start=True,
+                stop=True,
+            )
+
+        bias = keep.tile([P, GATES, HIDDEN], BF16)
+
+        def spread_bias(quarter):
+            gate, half = divmod(quarter, 2)
+            spread = work_psum.tile([P, 2, PIECE], BF16, tag="bank")
+            for s in range(2):
+                first = (2 * half + s) * PIECE
+                spread_row(spread[:, s, :], gate, slice(first, first + PIECE))
+            nc.scalar.copy(
+                out=bias[:, gate, 2 * half * PIECE : 2 * (half + 1) * PIECE],
+                in_=spread[:].rearrange("p s n -> p (s n)"),
+            )
+
+        pre = [keep.tile([P, HIDDEN], F32, name="pre%d" % gate) for gate in range(GATES)]
+        stats = [keep.tile([P, GROUPS, STATS], F32, name="stats%d" % gate) for gate in range(GATES)]
+        mean_var = [keep.tile([P, 2], F32, name="mean_var%d" % gate) for gate in range(GATES)]
+        var_eps = [keep.tile([P, 1], F32, name="var_eps%d" % gate) for gate in range(GATES)]
+        rstd = [keep.tile([P, 1], F32, name="rstd%d" % gate) for gate in range(GATES)]
+
+        raw_words = {}
+        w_grouped = {}
+        w_codes = {}
+        w_scales = {}
+        acc = {}
+        gain_shift = {}
+
+        def place(r):
+            gate, rest = divmod(r, GROUPS * OPERANDS)
+            group, operand = divmod(rest, OPERANDS)
+            return gate, group, operand
+
+        def load(r):
+            gate, group, operand = place(r)
+            raw = raw_pool.tile([P, 2 * FEATURES], BF16)
+            nc.sync.dma_start(
+                out=raw[:],
+                in_=weights[gate][operand][group * N_TILE : (group + 1) * N_TILE, :].rearrange(
+                    "(p a) k -> p (a k)", a=2
+                ),
+            )
+            raw_words[r] = raw[:].bitcast(F32)
+            codes = mx_pool.tile([P, PASSES * N_TILE], U32, align_bytes=64)
+            scales = mx_pool.tile([P, PASSES * N_TILE], U8, align_bytes=64)
+            w_codes[r] = codes
+            w_scales[r] = scales
+
+        def regroup(r, half):
+            grouped = grouped_pool.tile([P, 2 * N_TILE * PACK], BF16, align_bytes=64)
+            w_grouped[r, half] = grouped
+            grouped_words = grouped[:].bitcast(F32)
+            for s in range(2):
+                g = 2 * half + s
+                first = g * PASS_WORDS
+                on_vector = (r * PASSES + g) % VECTOR_EVERY == VECTOR_BANK
+                words_onto_partitions(
+                    nc,
+                    work_psum,
+                    identity_words[:],
+                    [raw_words[r][:, a * ROW_WORDS + first : a * ROW_WORDS + first + PASS_WORDS] for a in range(2)],
+                    grouped_words[:, s * BANK_WORDS : (s + 1) * BANK_WORDS],
+                    nc.vector.tensor_copy if on_vector else nc.scalar.copy,
+                )
+
+        def quantise(r, half):
+            cols = slice(2 * half * N_TILE, 2 * (half + 1) * N_TILE)
+            nc.vector.quantize_mx(
+                out=w_codes[r][:, cols].bitcast(FP8X4), scales=w_scales[r][:, cols], in_=w_grouped[r, half][:]
+            )
+
+        def multiply(r):
+            gate, group, operand = place(r)
+            if operand == 0:
+                bank = acc_psum.tile([P, N_TILE], F32, tag="acc")
+                acc[gate, group] = bank
+            for g in range(PASSES):
+                a_cols = slice((operand * PASSES + g) * P, (operand * PASSES + g + 1) * P)
+                w_cols = slice(g * N_TILE, (g + 1) * N_TILE)
+                nc.tensor.matmul_mx(
+                    out=acc[gate, group][:],
+                    lhsT=a_codes[:, a_cols].bitcast(FP8X4),
+                    lhsT_scale=a_scales[:, a_cols],
+                    rhs=w_codes[r][:, w_cols].bitcast(FP8X4),
+                    rhs_scale=w_scales[r][:, w_cols],
+                    start=(operand == 0 and g == 0),
+                    stop=(operand == OPERANDS - 1 and g == PASSES - 1),
+                )
+            if operand == OPERANDS - 1:
+                cols = slice(group * N_TILE, (group + 1) * N_TILE)
+                nc.vector.tensor_tensor(
+                    out=pre[gate][:, cols].rearrange("p (r a) -> p r a", a=2),
+                    in0=acc[gate, group][:].rearrange("p (a r) -> p r a", a=2),
+                    in1=bias[:, gate, cols].rearrange("p (r a) -> p r a", a=2),
+                    op=ALU.add,
+                )
+                nc.vector.bn_stats(out=stats[gate][:, group, :], in_=pre[gate][:, cols])
+
+        def moments(gate):
+            nc.vector.bn_aggr(out=mean_var[gate][:], in_=stats[gate][:].rearrange("p g s -> p (g s)"))
+            nc.vector.tensor_scalar(
+                out=var_eps[gate][:], in0=mean_var[gate][:, 1:2], scalar1=EPS, scalar2=None, op0=ALU.add
+            )
+            nc.gpsimd.tensor_tensor(out=rstd[gate][:], in0=var_eps[gate][:], in1=minus_half[:], op=ALU.pow)
+
+        def centre(gate, piece):
+            cols = slice(piece * PIECE, (piece + 1) * PIECE)
+            spread = work_psum.tile([P, 2, PIECE], BF16, tag="bank")
+            gain_shift[gate, piece] = spread
+            spread_row(spread[:, 0, :], 2 + 2 * gate, cols)
+            spread_row(spread[:, 1, :], 3 + 2 * gate, cols)
+            nc.vector.scalar_tensor_tensor(
+                out=pre[gate][:, cols],
+                in0=pre[gate][:, cols],
+                scalar=mean_var[gate][:, 0:1],
+                in1=spread[:, 0, :],
+                op0=ALU.subtract,
+                op1=ALU.mult,
+            )
+
+        def activate(gate, piece):
+            cols = slice(piece * PIECE, (piece + 1) * PIECE)
+            nc.vector.scalar_tensor_tensor(
+                out=pre[gate][:, cols],
+                in0=pre[gate][:, cols],
+                scalar=rstd[gate][:],
+                in1=gain_shift[gate, piece][:, 1, :],
+                op0=ALU.mult,
+                op1=ALU.add,
+            )
+            nc.scalar.activation(out=pre[gate][:, cols], in_=pre[gate][:, cols], func=functions[gate])
+
+        def product(piece):
+            cols = slice(piece * PIECE, (piece + 1) * PIECE)
+            engine = nc.gpsimd if piece < PIECES // 2 else nc.vector
+            engine.tensor_tensor(out=pre[1][:, cols], in0=pre[1][:, cols], in1=pre[0][:, cols], op=ALU.mult)
+            nc.sync.dma_start(out=out[:, cols], in_=pre[1][:, cols])
+
+        for r in range(ROUNDS):
+            load(r)
+            regroup(r, 0)
+            if r > 0:
+                quantise(r - 1, 1)
+            regroup(r, 1)
+            quantise(r, 0)
+            if r < GATES * 2:
+                spread_bias(r)
+            if r >= MX_LAG:
+                multiply(r - MX_LAG)
+            since_gate_0 = r - MX_LAG - (ROUNDS // GATES - 1)
+            if since_gate_0 == 0:
+                moments(0)
+            if since_gate_0 > 0 and since_gate_0 % 2 == 1 and since_gate_0 // 2 < PIECES:
+                centre(0, since_gate_0 // 2)
+                activate(0, since_gate_0 // 2)
+        quantise(ROUNDS - 1, 1)
+        for r in range(ROUNDS - MX_LAG, ROUNDS):
+            multiply(r)
+
+        moments(1)
+        for step in range(PIECES + 2):
+            if step < PIECES:
+                centre(1, step)
+            if 0 <= step - 1 < PIECES:
+                activate(1, step - 1)
+            if step - 2 >= 0:
+                product(step - 2)

@@ -31,7 +31,7 @@ STATS = 6
 EPS = 1e-5
 
 RAW_BUFS = 8
-MX_LAG = 2
+MX_LAG = 3
 VECTOR_EVERY = 8
 VECTOR_BANK = 5
 
@@ -61,8 +61,8 @@ def tile_layernormlstmcell_pa_kernel(
         ctx.enter_context(tc.manual_schedule())
         keep = ctx.enter_context(tc.tile_pool(name="keep", bufs=1))
         raw_pool = ctx.enter_context(tc.tile_pool(name="raw", bufs=RAW_BUFS))
-        grouped_pool = ctx.enter_context(tc.tile_pool(name="grouped", bufs=4))
-        mx_pool = ctx.enter_context(tc.tile_pool(name="mx", bufs=MX_LAG + 2))
+        grouped_pool = ctx.enter_context(tc.tile_pool(name="grouped", bufs=3))
+        mx_pool = ctx.enter_context(tc.tile_pool(name="mx", bufs=MX_LAG + 3))
         work_psum = ctx.enter_context(tc.psum_pool(name="work_psum", bufs=6))
         acc_psum = ctx.enter_context(tc.psum_pool(name="acc_psum", bufs=2))
 
@@ -79,8 +79,6 @@ def tile_layernormlstmcell_pa_kernel(
 
         vectors = keep.tile([P, HIDDEN], BF16)
         nc.vector.memset(vectors[:], 0.0)
-        for row, vector in enumerate(vector_rows):
-            nc.gpsimd.dma_start(out=vectors[row : row + 1, :], in_=vector.unsqueeze(0))
         minus_half = keep.tile([P, 1], F32)
         nc.vector.memset(minus_half[:], -0.5)
 
@@ -164,12 +162,11 @@ def tile_layernormlstmcell_pa_kernel(
             w_codes[r] = codes
             w_scales[r] = scales
 
-        def regroup(r, half):
-            grouped = grouped_pool.tile([P, 2 * N_TILE * PACK], BF16, align_bytes=64)
-            w_grouped[r, half] = grouped
+        def regroup(r):
+            grouped = grouped_pool.tile([P, PASSES * N_TILE * PACK], BF16, align_bytes=64)
+            w_grouped[r] = grouped
             grouped_words = grouped[:].bitcast(F32)
-            for s in range(2):
-                g = 2 * half + s
+            for g in range(PASSES):
                 first = g * PASS_WORDS
                 on_vector = (r * PASSES + g) % VECTOR_EVERY == VECTOR_BANK
                 words_onto_partitions(
@@ -177,15 +174,12 @@ def tile_layernormlstmcell_pa_kernel(
                     work_psum,
                     identity_words[:],
                     [raw_words[r][:, a * ROW_WORDS + first : a * ROW_WORDS + first + PASS_WORDS] for a in range(2)],
-                    grouped_words[:, s * BANK_WORDS : (s + 1) * BANK_WORDS],
+                    grouped_words[:, g * BANK_WORDS : (g + 1) * BANK_WORDS],
                     nc.vector.tensor_copy if on_vector else nc.scalar.copy,
                 )
 
-        def quantise(r, half):
-            cols = slice(2 * half * N_TILE, 2 * (half + 1) * N_TILE)
-            nc.vector.quantize_mx(
-                out=w_codes[r][:, cols].bitcast(FP8X4), scales=w_scales[r][:, cols], in_=w_grouped[r, half][:]
-            )
+        def quantise(r):
+            nc.vector.quantize_mx(out=w_codes[r][:].bitcast(FP8X4), scales=w_scales[r][:], in_=w_grouped[r][:])
 
         def multiply(r):
             gate, group, operand = place(r)
@@ -256,23 +250,25 @@ def tile_layernormlstmcell_pa_kernel(
 
         for r in range(ROUNDS):
             load(r)
-            regroup(r, 0)
+            if r == 1:
+                for row, vector in enumerate(vector_rows):
+                    nc.sync.dma_start(out=vectors[row : row + 1, :], in_=vector.unsqueeze(0))
+            regroup(r)
             if r > 0:
-                quantise(r - 1, 1)
-            regroup(r, 1)
-            quantise(r, 0)
-            if r < GATES * 2:
-                spread_bias(r)
-            if r >= MX_LAG:
-                multiply(r - MX_LAG)
-            since_gate_0 = r - MX_LAG - (ROUNDS // GATES - 1)
+                quantise(r - 1)
+            if 2 <= r < 2 + GATES * 2:
+                spread_bias(r - 2)
+            if r >= MX_LAG and r % OPERANDS == 1:
+                for operand in range(OPERANDS):
+                    multiply(r - MX_LAG + operand)
+            since_gate_0 = r - MX_LAG + 1 - (ROUNDS // GATES - 1)
             if since_gate_0 == 0:
                 moments(0)
             if since_gate_0 > 0 and since_gate_0 % 2 == 1 and since_gate_0 // 2 < PIECES:
                 centre(0, since_gate_0 // 2)
                 activate(0, since_gate_0 // 2)
-        quantise(ROUNDS - 1, 1)
-        for r in range(ROUNDS - MX_LAG, ROUNDS):
+        quantise(ROUNDS - 1)
+        for r in range(ROUNDS - MX_LAG + 1, ROUNDS):
             multiply(r)
 
         moments(1)

@@ -32,8 +32,7 @@ EPS = 1e-5
 
 RAW_BUFS = 8
 MX_LAG = 3
-VECTOR_EVERY = 8
-VECTOR_BANK = 5
+RELAID_PASS = PASSES - 1
 
 FLOPS = 2 * P * GATES * HIDDEN * OPERANDS * FEATURES
 
@@ -42,7 +41,7 @@ def words_onto_partitions(nc, psum, identity, blocks, dest, copy):
     bank = psum.tile([P, 2, 2, P], F32, tag="bank")
     for a in range(2):
         for u in range(2):
-            nc.tensor.transpose(bank[:, a, u, :], blocks[a][:, u : PASS_WORDS : 2], identity)
+            nc.tensor.transpose(bank[:, a, u, :], blocks[a][u], identity)
     copy(
         out=dest.rearrange("p (a r u) -> p a r u", a=2, u=2),
         in_=bank[:].rearrange("p a u r -> p a r u"),
@@ -61,6 +60,7 @@ def tile_layernormlstmcell_pa_kernel(
         ctx.enter_context(tc.manual_schedule())
         keep = ctx.enter_context(tc.tile_pool(name="keep", bufs=1))
         raw_pool = ctx.enter_context(tc.tile_pool(name="raw", bufs=RAW_BUFS))
+        relaid_pool = ctx.enter_context(tc.tile_pool(name="relaid", bufs=3))
         grouped_pool = ctx.enter_context(tc.tile_pool(name="grouped", bufs=3))
         mx_pool = ctx.enter_context(tc.tile_pool(name="mx", bufs=MX_LAG + 3))
         work_psum = ctx.enter_context(tc.psum_pool(name="work_psum", bufs=6))
@@ -98,7 +98,10 @@ def tile_layernormlstmcell_pa_kernel(
                     nc,
                     work_psum,
                     identity_words[:],
-                    [a_words[:, first + a * PASS_WORDS : first + (a + 1) * PASS_WORDS] for a in range(2)],
+                    [
+                        [a_words[:, first + a * PASS_WORDS + u : first + (a + 1) * PASS_WORDS : 2] for u in range(2)]
+                        for a in range(2)
+                    ],
                     a_grouped_words[:, first : first + BANK_WORDS],
                     nc.vector.tensor_copy if pair % 2 else nc.scalar.copy,
                 )
@@ -136,6 +139,7 @@ def tile_layernormlstmcell_pa_kernel(
         rstd = [keep.tile([P, 1], F32, name="rstd%d" % gate) for gate in range(GATES)]
 
         raw_words = {}
+        relaid = {}
         w_grouped = {}
         w_codes = {}
         w_scales = {}
@@ -162,20 +166,38 @@ def tile_layernormlstmcell_pa_kernel(
             w_codes[r] = codes
             w_scales[r] = scales
 
+        def relay(r):
+            words = relaid_pool.tile([P, 2, 2, P], F32)
+            row_words = raw_words[r].rearrange("p (a k) -> p a k", a=2)
+            nc.vector.tensor_copy(
+                out=words[:],
+                in_=row_words[:, :, RELAID_PASS * PASS_WORDS :].rearrange("p a (w u) -> p a u w", u=2),
+            )
+            relaid[r] = words
+
         def regroup(r):
             grouped = grouped_pool.tile([P, PASSES * N_TILE * PACK], BF16, align_bytes=64)
             w_grouped[r] = grouped
             grouped_words = grouped[:].bitcast(F32)
             for g in range(PASSES):
                 first = g * PASS_WORDS
-                on_vector = (r * PASSES + g) % VECTOR_EVERY == VECTOR_BANK
+                if g < RELAID_PASS:
+                    blocks = [
+                        [
+                            raw_words[r][:, a * ROW_WORDS + first + u : a * ROW_WORDS + first + PASS_WORDS : 2]
+                            for u in range(2)
+                        ]
+                        for a in range(2)
+                    ]
+                else:
+                    blocks = [[relaid[r][:, a, u, :] for u in range(2)] for a in range(2)]
                 words_onto_partitions(
                     nc,
                     work_psum,
                     identity_words[:],
-                    [raw_words[r][:, a * ROW_WORDS + first : a * ROW_WORDS + first + PASS_WORDS] for a in range(2)],
+                    blocks,
                     grouped_words[:, g * BANK_WORDS : (g + 1) * BANK_WORDS],
-                    nc.vector.tensor_copy if on_vector else nc.scalar.copy,
+                    nc.scalar.copy,
                 )
 
         def quantise(r):
@@ -248,14 +270,19 @@ def tile_layernormlstmcell_pa_kernel(
             engine.tensor_tensor(out=pre[1][:, cols], in0=pre[1][:, cols], in1=pre[0][:, cols], op=ALU.mult)
             nc.sync.dma_start(out=out[:, cols], in_=pre[1][:, cols])
 
+        load(0)
+        relay(0)
         for r in range(ROUNDS):
-            load(r)
-            if r == 1:
+            if r + 1 < ROUNDS:
+                load(r + 1)
+            if r == 0:
                 for row, vector in enumerate(vector_rows):
                     nc.sync.dma_start(out=vectors[row : row + 1, :], in_=vector.unsqueeze(0))
             regroup(r)
             if r > 0:
                 quantise(r - 1)
+            if r + 1 < ROUNDS:
+                relay(r + 1)
             if 2 <= r < 2 + GATES * 2:
                 spread_bias(r - 2)
             if r >= MX_LAG and r % OPERANDS == 1:

@@ -32,6 +32,8 @@ EPS = 1e-5
 
 RAW_BUFS = 8
 MX_LAG = 3
+VECTOR_EVERY = 8
+VECTOR_BANK = 5
 RELAID_PASS = PASSES - 1
 
 FLOPS = 2 * P * GATES * HIDDEN * OPERANDS * FEATURES
@@ -63,8 +65,8 @@ def tile_layernormlstmcell_pa_kernel(
         relaid_pool = ctx.enter_context(tc.tile_pool(name="relaid", bufs=3))
         grouped_pool = ctx.enter_context(tc.tile_pool(name="grouped", bufs=3))
         mx_pool = ctx.enter_context(tc.tile_pool(name="mx", bufs=MX_LAG + 3))
-        work_psum = ctx.enter_context(tc.psum_pool(name="work_psum", bufs=6))
-        acc_psum = ctx.enter_context(tc.psum_pool(name="acc_psum", bufs=2))
+        work_psum = ctx.enter_context(tc.psum_pool(name="work_psum", bufs=7))
+        acc_psum = ctx.enter_context(tc.psum_pool(name="acc_psum", bufs=1))
 
         a_raw = []
         for s, operand in enumerate((x, h)):
@@ -197,7 +199,7 @@ def tile_layernormlstmcell_pa_kernel(
                     identity_words[:],
                     blocks,
                     grouped_words[:, g * BANK_WORDS : (g + 1) * BANK_WORDS],
-                    nc.scalar.copy,
+                    nc.vector.tensor_copy if (r * PASSES + g) % VECTOR_EVERY == VECTOR_BANK else nc.scalar.copy,
                 )
 
         def quantise(r):

@@ -34,6 +34,8 @@ RAW_BUFS = 8
 MX_LAG = 3
 VECTOR_EVERY = 8
 VECTOR_BANK = 5
+RELAY_LEAD = 2
+FIRST_RELAID = 3
 RELAID_PASS = PASSES - 1
 
 FLOPS = 2 * P * GATES * HIDDEN * OPERANDS * FEATURES
@@ -62,7 +64,7 @@ def tile_layernormlstmcell_pa_kernel(
         ctx.enter_context(tc.manual_schedule())
         keep = ctx.enter_context(tc.tile_pool(name="keep", bufs=1))
         raw_pool = ctx.enter_context(tc.tile_pool(name="raw", bufs=RAW_BUFS))
-        relaid_pool = ctx.enter_context(tc.tile_pool(name="relaid", bufs=3))
+        relaid_pool = ctx.enter_context(tc.tile_pool(name="relaid", bufs=RELAY_LEAD + 2))
         grouped_pool = ctx.enter_context(tc.tile_pool(name="grouped", bufs=3))
         mx_pool = ctx.enter_context(tc.tile_pool(name="mx", bufs=MX_LAG + 3))
         work_psum = ctx.enter_context(tc.psum_pool(name="work_psum", bufs=7))
@@ -71,7 +73,9 @@ def tile_layernormlstmcell_pa_kernel(
         a_raw = []
         for s, operand in enumerate((x, h)):
             rows = keep.tile([P, FEATURES], BF16, name="a_raw%d" % s)
-            nc.sync.dma_start(out=rows[:], in_=operand)
+            for half in range(2):
+                cols = slice(half * FEATURES // 2, (half + 1) * FEATURES // 2)
+                nc.sync.dma_start(out=rows[:, cols], in_=operand[:, cols])
             a_raw.append(rows)
 
         identity_words = keep.tile([P, P], F32)
@@ -156,12 +160,13 @@ def tile_layernormlstmcell_pa_kernel(
         def load(r):
             gate, group, operand = place(r)
             raw = raw_pool.tile([P, 2 * FEATURES], BF16)
-            nc.sync.dma_start(
-                out=raw[:],
-                in_=weights[gate][operand][group * N_TILE : (group + 1) * N_TILE, :].rearrange(
-                    "(p a) k -> p (a k)", a=2
-                ),
-            )
+            pieces = 2 if r < 2 else 1
+            source = weights[gate][operand][group * N_TILE : (group + 1) * N_TILE, :].rearrange("(p a) k -> p a k", a=2)
+            for piece in range(pieces):
+                cols = slice(piece * FEATURES // pieces, (piece + 1) * FEATURES // pieces)
+                nc.sync.dma_start(
+                    out=raw[:].rearrange("p (a k) -> p a k", a=2)[:, :, cols], in_=source[:, :, cols]
+                )
             raw_words[r] = raw[:].bitcast(F32)
             codes = mx_pool.tile([P, PASSES * N_TILE], U32, align_bytes=64)
             scales = mx_pool.tile([P, PASSES * N_TILE], U8, align_bytes=64)
@@ -183,7 +188,7 @@ def tile_layernormlstmcell_pa_kernel(
             grouped_words = grouped[:].bitcast(F32)
             for g in range(PASSES):
                 first = g * PASS_WORDS
-                if g < RELAID_PASS:
+                if g < RELAID_PASS or r < FIRST_RELAID:
                     blocks = [
                         [
                             raw_words[r][:, a * ROW_WORDS + first + u : a * ROW_WORDS + first + PASS_WORDS : 2]
@@ -202,8 +207,13 @@ def tile_layernormlstmcell_pa_kernel(
                     nc.vector.tensor_copy if (r * PASSES + g) % VECTOR_EVERY == VECTOR_BANK else nc.scalar.copy,
                 )
 
-        def quantise(r):
-            nc.vector.quantize_mx(out=w_codes[r][:].bitcast(FP8X4), scales=w_scales[r][:], in_=w_grouped[r][:])
+        def quantise(r, parts=1):
+            for part in range(parts):
+                cols = slice(part * PASSES * N_TILE // parts, (part + 1) * PASSES * N_TILE // parts)
+                values = slice(cols.start * PACK, cols.stop * PACK)
+                nc.vector.quantize_mx(
+                    out=w_codes[r][:, cols].bitcast(FP8X4), scales=w_scales[r][:, cols], in_=w_grouped[r][:, values]
+                )
 
         def multiply(r):
             gate, group, operand = place(r)
@@ -239,17 +249,20 @@ def tile_layernormlstmcell_pa_kernel(
             )
             nc.gpsimd.tensor_tensor(out=rstd[gate][:], in0=var_eps[gate][:], in1=minus_half[:], op=ALU.pow)
 
-        def centre(gate, piece):
+        def spread_gain_shift(gate, piece):
             cols = slice(piece * PIECE, (piece + 1) * PIECE)
             spread = work_psum.tile([P, 2, PIECE], BF16, tag="bank")
             gain_shift[gate, piece] = spread
             spread_row(spread[:, 0, :], 2 + 2 * gate, cols)
             spread_row(spread[:, 1, :], 3 + 2 * gate, cols)
+
+        def centre(gate, piece):
+            cols = slice(piece * PIECE, (piece + 1) * PIECE)
             nc.vector.scalar_tensor_tensor(
                 out=pre[gate][:, cols],
                 in0=pre[gate][:, cols],
                 scalar=mean_var[gate][:, 0:1],
-                in1=spread[:, 0, :],
+                in1=gain_shift[gate, piece][:, 0, :],
                 op0=ALU.subtract,
                 op1=ALU.mult,
             )
@@ -272,19 +285,19 @@ def tile_layernormlstmcell_pa_kernel(
             engine.tensor_tensor(out=pre[1][:, cols], in0=pre[1][:, cols], in1=pre[0][:, cols], op=ALU.mult)
             nc.sync.dma_start(out=out[:, cols], in_=pre[1][:, cols])
 
-        load(0)
-        relay(0)
+        for r in range(RELAY_LEAD):
+            load(r)
         for r in range(ROUNDS):
-            if r + 1 < ROUNDS:
-                load(r + 1)
+            if r + RELAY_LEAD < ROUNDS:
+                load(r + RELAY_LEAD)
             if r == 0:
                 for row, vector in enumerate(vector_rows):
                     nc.sync.dma_start(out=vectors[row : row + 1, :], in_=vector.unsqueeze(0))
             regroup(r)
             if r > 0:
                 quantise(r - 1)
-            if r + 1 < ROUNDS:
-                relay(r + 1)
+            if FIRST_RELAID <= r + RELAY_LEAD < ROUNDS:
+                relay(r + RELAY_LEAD)
             if 2 <= r < 2 + GATES * 2:
                 spread_bias(r - 2)
             if r >= MX_LAG and r % OPERANDS == 1:
@@ -294,11 +307,14 @@ def tile_layernormlstmcell_pa_kernel(
             if since_gate_0 == 0:
                 moments(0)
             if since_gate_0 > 0 and since_gate_0 % 2 == 1 and since_gate_0 // 2 < PIECES:
+                spread_gain_shift(0, since_gate_0 // 2)
                 centre(0, since_gate_0 // 2)
                 activate(0, since_gate_0 // 2)
-        quantise(ROUNDS - 1)
-        for r in range(ROUNDS - MX_LAG + 1, ROUNDS):
-            multiply(r)
+        quantise(ROUNDS - 1, parts=2)
+        for half in range(2):
+            multiply(ROUNDS - 2 + half)
+            for piece in range(half * PIECES // 2, (half + 1) * PIECES // 2):
+                spread_gain_shift(1, piece)
 
         moments(1)
         for step in range(PIECES + 2):

from contextlib import ExitStack

import concourse.mybir as mybir
from concourse.masks import make_identity

F32 = mybir.dt.float32
BF16 = mybir.dt.bfloat16
U32 = mybir.dt.uint32
U8 = mybir.dt.uint8
FP8X4 = mybir.dt.float8_e4m3fn_x4
ALU = mybir.AluOpType
ACT = mybir.ActivationFunctionType

P = 128
FEATURES = 2048
HIDDEN = 2048
GATES = 2
OPERANDS = 2
PACK = 4
K_PASS = P * PACK
PASSES = FEATURES // K_PASS
PASS_WORDS = K_PASS // 2
ROW_WORDS = FEATURES // 2
N_TILE = 2 * P
GROUPS = HIDDEN // N_TILE
ROUNDS = GATES * GROUPS * OPERANDS
BANK_WORDS = 512
PIECE = 512
PIECES = HIDDEN // PIECE
STATS = 6
EPS = 1e-5

RAW_BUFS = 8
MX_LAG = 3
VECTOR_EVERY = 8
VECTOR_BANK = 5
RELAY_LEAD = 2
FIRST_RELAID = 3
RELAID_PASS = PASSES - 1

FLOPS = 2 * P * GATES * HIDDEN * OPERANDS * FEATURES


def words_onto_partitions(nc, psum, identity, blocks, dest, copy):
    bank = psum.tile([P, 2, 2, P], F32, tag="bank")
    for a in range(2):
        for u in range(2):
            nc.tensor.transpose(bank[:, a, u, :], blocks[a][u], identity)
    copy(
        out=dest.rearrange("p (a r u) -> p a r u", a=2, u=2),
        in_=bank[:].rearrange("p a u r -> p a r u"),
    )


def tile_layernormlstmcell_pa_kernel(
    tc, x, h, Wi_w, Wi_b, Ui_w, lni_g, lni_b, Wc_w, Wc_b, Uc_w, lnc_g, lnc_b, out
):
    nc = tc.nc
    weights = ((Wi_w, Ui_w), (Wc_w, Uc_w))
    vector_rows = (Wi_b, Wc_b, lni_g, lni_b, lnc_g, lnc_b)
    functions = (ACT.Sigmoid, ACT.Tanh)

    with ExitStack() as ctx:
        ctx.enter_context(tc.manual_schedule())
        keep = ctx.enter_context(tc.tile_pool(name="keep", bufs=1))
        raw_pool = ctx.enter_context(tc.tile_pool(name="raw", bufs=RAW_BUFS))
        relaid_pool = ctx.enter_context(tc.tile_pool(name="relaid", bufs=RELAY_LEAD + 2))
        grouped_pool = ctx.enter_context(tc.tile_pool(name="grouped", bufs=3))
        mx_pool = ctx.enter_context(tc.tile_pool(name="mx", bufs=MX_LAG + 3))
        work_psum = ctx.enter_context(tc.psum_pool(name="work_psum", bufs=7))
        acc_psum = ctx.enter_context(tc.psum_pool(name="acc_psum", bufs=1))

        a_raw = []
        for s, operand in enumerate((x, h)):
            rows = keep.tile([P, FEATURES], BF16, name="a_raw%d" % s)
            for half in range(2):
                cols = slice(half * FEATURES // 2, (half + 1) * FEATURES // 2)
                nc.sync.dma_start(out=rows[:, cols], in_=operand[:, cols])
            a_raw.append(rows)

        identity_words = keep.tile([P, P], F32)
        make_identity(nc, identity_words[:])
        identity_bf16 = keep.tile([P, P], BF16)
        make_identity(nc, identity_bf16[:])

        vectors = keep.tile([P, HIDDEN], BF16)
        nc.vector.memset(vectors[:], 0.0)
        minus_half = keep.tile([P, 1], F32)
        nc.vector.memset(minus_half[:], -0.5)

        table_warmer = keep.tile([P, 1], F32)
        nc.vector.memset(table_warmer[:], 0.0)
        nc.scalar.activation(out=table_warmer[:], in_=table_warmer[:], func=ACT.Sigmoid)

        a_codes = keep.tile([P, OPERANDS * PASSES * P], U32, align_bytes=64)
        a_scales = keep.tile([P, OPERANDS * PASSES * P], U8, align_bytes=64)
        for s in range(OPERANDS):
            a_words = a_raw[s][:].bitcast(F32)
            a_grouped = keep.tile([P, PASSES * P * PACK], BF16, align_bytes=64, name="a_grouped%d" % s)
            a_grouped_words = a_grouped[:].bitcast(F32)
            for pair in range(PASSES // 2):
                first = 2 * pair * PASS_WORDS
                words_onto_partitions(
                    nc,
                    work_psum,
                    identity_words[:],
                    [
                        [a_words[:, first + a * PASS_WORDS + u : first + (a + 1) * PASS_WORDS : 2] for u in range(2)]
                        for a in range(2)
                    ],
                    a_grouped_words[:, first : first + BANK_WORDS],
                    nc.vector.tensor_copy if pair % 2 else nc.scalar.copy,
                )
            a_cols = slice(s * PASSES * P, (s + 1) * PASSES * P)
            nc.vector.quantize_mx(
                out=a_codes[:, a_cols].bitcast(FP8X4), scales=a_scales[:, a_cols], in_=a_grouped[:]
            )

        def spread_row(dest, row, cols):
            nc.tensor.matmul(
                out=dest,
                lhsT=identity_bf16[:, row : row + 1].to_broadcast([P, P]),
                rhs=vectors[:, cols],
                start=True,
                stop=True,
            )

        bias = keep.tile([P, GATES, HIDDEN], BF16)

        def spread_bias(quarter):
            gate, half = divmod(quarter, 2)
            spread = work_psum.tile([P, 2, PIECE], BF16, tag="bank")
            for s in range(2):
                first = (2 * half + s) * PIECE
                spread_row(spread[:, s, :], gate, slice(first, first + PIECE))
            nc.scalar.copy(
                out=bias[:, gate, 2 * half * PIECE : 2 * (half + 1) * PIECE],
                in_=spread[:].rearrange("p s n -> p (s n)"),
            )

        pre = [keep.tile([P, HIDDEN], F32, name="pre%d" % gate) for gate in range(GATES)]
        stats = [keep.tile([P, GROUPS, STATS], F32, name="stats%d" % gate) for gate in range(GATES)]
        mean_var = [keep.tile([P, 2], F32, name="mean_var%d" % gate) for gate in range(GATES)]
        var_eps = [keep.tile([P, 1], F32, name="var_eps%d" % gate) for gate in range(GATES)]
        rstd = [keep.tile([P, 1], F32, name="rstd%d" % gate) for gate in range(GATES)]

        raw_words = {}
        relaid = {}
        w_grouped = {}
        w_codes = {}
        w_scales = {}
        acc = {}
        gain_shift = {}

        def place(r):
            gate, rest = divmod(r, GROUPS * OPERANDS)
            group, operand = divmod(rest, OPERANDS)
            return gate, group, operand

        def load(r):
            gate, group, operand = place(r)
            raw = raw_pool.tile([P, 2 * FEATURES], BF16)
            pieces = 2 if r < 2 else 1
            source = weights[gate][operand][group * N_TILE : (group + 1) * N_TILE, :].rearrange("(p a) k -> p a k", a=2)
            for piece in range(pieces):
                cols = slice(piece * FEATURES // pieces, (piece + 1) * FEATURES // pieces)
                nc.sync.dma_start(
                    out=raw[:].rearrange("p (a k) -> p a k", a=2)[:, :, cols], in_=source[:, :, cols]
                )
            raw_words[r] = raw[:].bitcast(F32)
            codes = mx_pool.tile([P, PASSES * N_TILE], U32, align_bytes=64)
            scales = mx_pool.tile([P, PASSES * N_TILE], U8, align_bytes=64)
            w_codes[r] = codes
            w_scales[r] = scales

        def relay(r):
            words = relaid_pool.tile([P, 2, 2, P], F32)
            row_words = raw_words[r].rearrange("p (a k) -> p a k", a=2)
            nc.vector.tensor_copy(
                out=words[:],
                in_=row_words[:, :, RELAID_PASS * PASS_WORDS :].rearrange("p a (w u) -> p a u w", u=2),
            )
            relaid[r] = words

        def regroup(r):
            grouped = grouped_pool.tile([P, PASSES * N_TILE * PACK], BF16, align_bytes=64)
            w_grouped[r] = grouped
            grouped_words = grouped[:].bitcast(F32)
            for g in range(PASSES):
                first = g * PASS_WORDS
                if g < RELAID_PASS or r < FIRST_RELAID:
                    blocks = [
                        [
                            raw_words[r][:, a * ROW_WORDS + first + u : a * ROW_WORDS + first + PASS_WORDS : 2]
                            for u in range(2)
                        ]
                        for a in range(2)
                    ]
                else:
                    blocks = [[relaid[r][:, a, u, :] for u in range(2)] for a in range(2)]
                words_onto_partitions(
                    nc,
                    work_psum,
                    identity_words[:],
                    blocks,
                    grouped_words[:, g * BANK_WORDS : (g + 1) * BANK_WORDS],
                    nc.vector.tensor_copy if (r * PASSES + g) % VECTOR_EVERY == VECTOR_BANK else nc.scalar.copy,
                )

        def quantise(r, parts=1):
            for part in range(parts):
                cols = slice(part * PASSES * N_TILE // parts, (part + 1) * PASSES * N_TILE // parts)
                values = slice(cols.start * PACK, cols.stop * PACK)
                nc.vector.quantize_mx(
                    out=w_codes[r][:, cols].bitcast(FP8X4), scales=w_scales[r][:, cols], in_=w_grouped[r][:, values]
                )

        def multiply(r):
            gate, group, operand = place(r)
            if operand == 0:
                bank = acc_psum.tile([P, N_TILE], F32, tag="acc")
                acc[gate, group] = bank
            for g in range(PASSES):
                a_cols = slice((operand * PASSES + g) * P, (operand * PASSES + g + 1) * P)
                w_cols = slice(g * N_TILE, (g + 1) * N_TILE)
                nc.tensor.matmul_mx(
                    out=acc[gate, group][:],
                    lhsT=a_codes[:, a_cols].bitcast(FP8X4),
                    lhsT_scale=a_scales[:, a_cols],
                    rhs=w_codes[r][:, w_cols].bitcast(FP8X4),
                    rhs_scale=w_scales[r][:, w_cols],
                    start=(operand == 0 and g == 0),
                    stop=(operand == OPERANDS - 1 and g == PASSES - 1),
                )
            if operand == OPERANDS - 1:
                cols = slice(group * N_TILE, (group + 1) * N_TILE)
                nc.vector.tensor_tensor(
                    out=pre[gate][:, cols].rearrange("p (r a) -> p r a", a=2),
                    in0=acc[gate, group][:].rearrange("p (a r) -> p r a", a=2),
                    in1=bias[:, gate, cols].rearrange("p (r a) -> p r a", a=2),
                    op=ALU.add,
                )
                nc.vector.bn_stats(out=stats[gate][:, group, :], in_=pre[gate][:, cols])

        def moments(gate):
            nc.vector.bn_aggr(out=mean_var[gate][:], in_=stats[gate][:].rearrange("p g s -> p (g s)"))
            nc.vector.tensor_scalar(
                out=var_eps[gate][:], in0=mean_var[gate][:, 1:2], scalar1=EPS, scalar2=None, op0=ALU.add
            )
            nc.gpsimd.tensor_tensor(out=rstd[gate][:], in0=var_eps[gate][:], in1=minus_half[:], op=ALU.pow)

        def spread_gain_shift(gate, piece):
            cols = slice(piece * PIECE, (piece + 1) * PIECE)
            spread = work_psum.tile([P, 2, PIECE], BF16, tag="bank")
            gain_shift[gate, piece] = spread
            spread_row(spread[:, 0, :], 2 + 2 * gate, cols)
            spread_row(spread[:, 1, :], 3 + 2 * gate, cols)

        def centre(gate, piece):
            cols = slice(piece * PIECE, (piece + 1) * PIECE)
            nc.vector.scalar_tensor_tensor(
                out=pre[gate][:, cols],
                in0=pre[gate][:, cols],
                scalar=mean_var[gate][:, 0:1],
                in1=gain_shift[gate, piece][:, 0, :],
                op0=ALU.subtract,
                op1=ALU.mult,
            )

        def activate(gate, piece):
            cols = slice(piece * PIECE, (piece + 1) * PIECE)
            nc.vector.scalar_tensor_tensor(
                out=pre[gate][:, cols],
                in0=pre[gate][:, cols],
                scalar=rstd[gate][:],
                in1=gain_shift[gate, piece][:, 1, :],
                op0=ALU.mult,
                op1=ALU.add,
            )
            nc.scalar.activation(out=pre[gate][:, cols], in_=pre[gate][:, cols], func=functions[gate])

        def product(piece):
            cols = slice(piece * PIECE, (piece + 1) * PIECE)
            engine = nc.gpsimd if piece < PIECES // 2 else nc.vector
            engine.tensor_tensor(out=pre[1][:, cols], in0=pre[1][:, cols], in1=pre[0][:, cols], op=ALU.mult)
            nc.sync.dma_start(out=out[:, cols], in_=pre[1][:, cols])

        for r in range(RELAY_LEAD):
            load(r)
        for r in range(ROUNDS):
            if r + RELAY_LEAD < ROUNDS:
                load(r + RELAY_LEAD)
            if r == 0:
                for row, vector in enumerate(vector_rows):
                    nc.sync.dma_start(out=vectors[row : row + 1, :], in_=vector.unsqueeze(0))
            regroup(r)
            if r > 0:
                quantise(r - 1)
            if FIRST_RELAID <= r + RELAY_LEAD < ROUNDS:
                relay(r + RELAY_LEAD)
            if 2 <= r < 2 + GATES * 2:
                spread_bias(r - 2)
            if r >= MX_LAG and r % OPERANDS == 1:
                for operand in range(OPERANDS):
                    multiply(r - MX_LAG + operand)
            since_gate_0 = r - MX_LAG + 1 - (ROUNDS // GATES - 1)
            if since_gate_0 == 0:
                moments(0)
            if since_gate_0 > 0 and since_gate_0 % 2 == 1 and since_gate_0 // 2 < PIECES:
                spread_gain_shift(0, since_gate_0 // 2)
                centre(0, since_gate_0 // 2)
                activate(0, since_gate_0 // 2)
        quantise(ROUNDS - 1, parts=2)
        for half in range(2):
            multiply(ROUNDS - 2 + half)
            for piece in range(half * PIECES // 2, (half + 1) * PIECES // 2):
                spread_gain_shift(1, piece)

        moments(1)
        for step in range(PIECES + 2):
            if step < PIECES:
                centre(1, step)
            if 0 <= step - 1 < PIECES:
                activate(1, step - 1)
            if step - 2 >= 0:
                product(step - 2)
